import numpy as np
import ml_dtypes


def mxq(x, axis, fmt="e4m3"):
    dtype, down = {"e4m3": (ml_dtypes.float8_e4m3fn, 7), "e5m2": (ml_dtypes.float8_e5m2, 14)}[fmt]
    v = np.moveaxis(np.asarray(x, np.float32).astype(ml_dtypes.bfloat16).astype(np.float64), axis, -1)
    blocks = v.reshape(v.shape[:-1] + (-1, 32))
    amax = np.abs(blocks).max(-1, keepdims=True)
    byte = np.maximum(np.where(amax > 0, np.frexp(amax)[1] - 1 + 127, 0) - down, 1)
    scale = np.exp2(byte - 127.0)
    codes = (blocks / scale).astype(np.float32).astype(dtype).astype(np.float64)
    return np.moveaxis((codes * scale).reshape(v.shape), -1, axis)


WIDE = False


def mx_kscale(k):
    if not WIDE:
        return np.ones(k)
    levels = np.array([10, -10, 5, -5, 0])
    a = np.random.permutation(np.resize(levels, k // 512 * 4)).reshape(k // 512, 4)
    idx = np.arange(k)
    return np.exp2(a[idx // 512, idx % 128 // 32])


BF16 = ml_dtypes.bfloat16


def bf(x):
    return np.asarray(x, np.float32).astype(BF16)


def f64(x):
    return np.asarray(x).astype(np.float64)


B, C, N = 2, 4, 512
NH = N // 2


def setup_inputs():
    u = np.where(np.arange(N) < NH, 1.0, mx_kscale(N))
    return {"x": bf(np.random.standard_normal((B, C, N, N)) * u),
            "haar": bf(np.random.standard_normal((N, N)) / np.sqrt(N) * u[None, :] / u[:, None])}


def reference(x, haar):
    r = f64(x).transpose(0, 2, 1, 3).reshape(B, C, N, N)[:, :, :NH, :]
    hq = mxq(f64(haar), 0, "e4m3")
    t = mxq(r, 3, "e4m3") @ hq
    return mxq(t, 3, "e4m3") @ hq[:, :NH]

@@ -1,0 +1,179 @@
+from contextlib import ExitStack
+
+import concourse.bass as bass
+import concourse.mybir as mybir
+import concourse.tile as tile
+from concourse.masks import make_identity
+
+FP8X4 = mybir.dt.float8_e4m3fn_x4
+BF16 = mybir.dt.bfloat16
+F32 = mybir.dt.float32
+U32 = mybir.dt.uint32
+U8 = mybir.dt.uint8
+
+P = 128
+FLOPS = 2 * 2048 * 512 * 512 + 2 * 2048 * 512 * 256
+BYTES = 2048 * 512 * 2 + 512 * 512 * 2 + 2048 * 256 * 4
+
+MANUAL = False
+EO_ON_VECTOR = (6, 7)
+ER_ON_SCALAR = (0, 1)
+
+
+def tile_mylayer_kernel(tc, x, haar, out):
+    nc = tc.nc
+    with ExitStack() as ctx:
+        keep = ctx.enter_context(tc.tile_pool(name="keep", bufs=1))
+        ps_rt = ctx.enter_context(tc.psum_pool(name="ps_rt", bufs=2))
+        ps_t = ctx.enter_context(tc.psum_pool(name="ps_t", bufs=4))
+        ps_o = ctx.enter_context(tc.psum_pool(name="ps_o", bufs=2))
+        if MANUAL:
+            ctx.enter_context(tc.manual_schedule())
+
+        ident = keep.tile([P, P], F32, name="ident")
+        haar_sb = keep.tile([P, 2048], BF16, name="haar_sb")
+        hg = keep.tile([P, 2048], BF16, name="hg", align_bytes=64)
+        h1c = keep.tile([P, 512], U32, name="h1c", align_bytes=64)
+        h1s = keep.tile([P, 512], U8, name="h1s", align_bytes=64)
+        h2c = keep.tile([P, 256], U32, name="h2c", align_bytes=64)
+        h2s = keep.tile([P, 256], U8, name="h2s", align_bytes=64)
+        xs = [keep.tile([P, 2048], BF16, name="x%d" % c) for c in range(4)]
+        gr = [keep.tile([P, 2048], BF16, name="gr%d" % c, align_bytes=64) for c in range(4)]
+        rc = [keep.tile([P, 512], U32, name="rc%d" % c, align_bytes=64) for c in range(4)]
+        rs = [keep.tile([P, 512], U8, name="rs%d" % c, align_bytes=64) for c in range(4)]
+        gt = [keep.tile([P, 2048], BF16, name="gt%d" % c, align_bytes=64) for c in range(4)]
+        tcd = [keep.tile([P, 512], U32, name="tc%d" % c, align_bytes=64) for c in range(4)]
+        tsc = [keep.tile([P, 512], U8, name="ts%d" % c, align_bytes=64) for c in range(4)]
+        ob = [keep.tile([P, 1024], F32, name="ob%d" % c) for c in range(4)]
+
+        def load_x(c, ch0, nch):
+            b, c2p = divmod(c, 2)
+            for c2i in range(2):
+                r0 = 128 * (2 * c2p + c2i)
+                nc.sync.dma_start(
+                    out=xs[c][c2i:P:2, 512 * ch0 : 512 * (ch0 + nch)].rearrange("p (ch k) -> p ch k", ch=nch),
+                    in_=x[b, ch0 : ch0 + nch, r0 : r0 + 64, :].rearrange("ch r k -> r ch k"),
+                )
+
+        def load_haar():
+            nc.sync.dma_start(
+                out=haar_sb[:].rearrange("p (t n) -> p t n", t=4),
+                in_=haar.rearrange("(p t) n -> p t n", t=4),
+            )
+
+        def prep_haar():
+            nc.vector.tensor_copy(
+                out=hg[:].rearrange("p (j c t) -> p j c t", j=4, t=4),
+                in_=haar_sb[:].rearrange("p (t c j) -> p j c t", t=4, j=4),
+            )
+            nc.vector.quantize_mx(out=h1c[:].bitcast(FP8X4), scales=h1s[:], in_=hg[:])
+
+        def prep_haar2():
+            for j in range(4):
+                nc.vector.quantize_mx(
+                    out=h2c[:, 64 * j : 64 * j + 64].bitcast(FP8X4),
+                    scales=h2s[:, 64 * j : 64 * j + 64],
+                    in_=hg[:, 512 * j : 512 * j + 256],
+                )
+
+        def stage_t(g):
+            c, h = divmod(g, 2)
+            rt = ps_rt.tile([P, 2, 256], F32, name="rt")
+            xw = xs[c][:].bitcast(F32)
+            for i in range(2):
+                ch = 2 * h + i
+                for u in range(2):
+                    nc.tensor.transpose(
+                        rt[:, u, 128 * i : 128 * i + 128],
+                        xw[:, 256 * ch + u : 256 * (ch + 1) : 2],
+                        ident[:],
+                    )
+            dst = gr[c][:].bitcast(F32)[:, 512 * h : 512 * h + 512].rearrange("p (m u) -> p m u", u=2)
+            src = rt[:].rearrange("p u m -> p m u")
+            if g in ER_ON_SCALAR:
+                nc.scalar.copy(out=dst, in_=src)
+            else:
+                nc.vector.tensor_copy(out=dst, in_=src)
+
+        def quant(g, src, codes, scales):
+            c, h = divmod(g, 2)
+            nc.vector.quantize_mx(
+                out=codes[c][:, 256 * h : 256 * h + 256].bitcast(FP8X4),
+                scales=scales[c][:, 256 * h : 256 * h + 256],
+                in_=src[c][:, 1024 * h : 1024 * h + 1024],
+            )
+
+        def stage_m1(g):
+            c, h = divmod(g, 2)
+            for i in range(2):
+                mo = 256 * h + 128 * i
+                tp = ps_t.tile([P, 4, 128], F32, name="tp")
+                for t in range(4):
+                    nc.tensor.matmul_mx(
+                        out=tp[:, t, :],
+                        lhsT=h1c[:, 128 * t : 128 * t + 128].bitcast(FP8X4),
+                        lhsT_scale=h1s[:, 128 * t : 128 * t + 128],
+                        rhs=rc[c][:, mo : mo + 128].bitcast(FP8X4),
+                        rhs_scale=rs[c][:, mo : mo + 128],
+                        start=True,
+                        stop=True,
+                    )
+                nc.scalar.copy(
+                    out=gt[c][:, 4 * mo : 4 * mo + 512].rearrange("p (m t) -> p m t", t=4),
+                    in_=tp[:].rearrange("p t m -> p m t"),
+                )
+
+        def stage_m2(g):
+            c, h = divmod(g, 2)
+            b, c2p = divmod(c, 2)
+            op = ps_o.tile([P, 2, 256], F32, name="op")
+            for i in range(2):
+                mo = 256 * h + 128 * i
+                nc.tensor.matmul_mx(
+                    out=op[:, i, :],
+                    lhsT=tcd[c][:, mo : mo + 128].bitcast(FP8X4),
+                    lhsT_scale=tsc[c][:, mo : mo + 128],
+                    rhs=h2c[:].bitcast(FP8X4),
+                    rhs_scale=h2s[:],
+                    start=True,
+                    stop=True,
+                )
+            dst = ob[c][:, 512 * h : 512 * h + 512].rearrange("p (i c j) -> p i c j", i=2, j=4)
+            src = op[:].rearrange("p i (j c) -> p i c j", j=4)
+            if g in EO_ON_VECTOR:
+                nc.vector.tensor_copy(out=dst, in_=src)
+            else:
+                nc.scalar.copy(out=dst, in_=src)
+            for c2i in range(2):
+                nc.sync.dma_start(
+                    out=out[b, 2 * c2p + c2i].rearrange("(r ch) j -> r ch j", ch=4)[:, 2 * h : 2 * h + 2, :],
+                    in_=ob[c][c2i:P:2, 512 * h : 512 * h + 512].rearrange("p (ch j) -> p ch j", ch=2),
+                )
+
+        make_identity(nc, ident[:])
+        load_x(0, 0, 2)
+        load_haar()
+        load_x(0, 2, 2)
+        for c in range(1, 4):
+            load_x(c, 0, 4)
+
+        stage_t(0)
+        prep_haar()
+        quant(0, gr, rc, rs)
+        stage_t(1)
+        quant(1, gr, rc, rs)
+        prep_haar2()
+        for s in range(0, 8, 2):
+            stage_m1(s)
+            stage_m1(s + 1)
+            if s + 2 < 8:
+                stage_t(s + 2)
+                stage_t(s + 3)
+            quant(s, gt, tcd, tsc)
+            if s + 2 < 8:
+                quant(s + 2, gr, rc, rs)
+            quant(s + 1, gt, tcd, tsc)
+            if s + 2 < 8:
+                quant(s + 3, gr, rc, rs)
+            stage_m2(s)
+            stage_m2(s + 1)

@@ -1,8 +1,6 @@
 from contextlib import ExitStack
 
-import concourse.bass as bass
 import concourse.mybir as mybir
-import concourse.tile as tile
 from concourse.masks import make_identity
 
 FP8X4 = mybir.dt.float8_e4m3fn_x4
@@ -15,44 +13,52 @@ P = 128
 FLOPS = 2 * 2048 * 512 * 512 + 2 * 2048 * 512 * 256
 BYTES = 2048 * 512 * 2 + 512 * 512 * 2 + 2048 * 256 * 4
 
-MANUAL = False
-EO_ON_VECTOR = (6, 7)
-ER_ON_SCALAR = (0, 1)
+MANUAL = True
+EO_ON_VECTOR = (0, 2, 6)
+RG_ON_SCALAR = 1
 
 
 def tile_mylayer_kernel(tc, x, haar, out):
     nc = tc.nc
     with ExitStack() as ctx:
         keep = ctx.enter_context(tc.tile_pool(name="keep", bufs=1))
-        ps_rt = ctx.enter_context(tc.psum_pool(name="ps_rt", bufs=2))
-        ps_t = ctx.enter_context(tc.psum_pool(name="ps_t", bufs=4))
-        ps_o = ctx.enter_context(tc.psum_pool(name="ps_o", bufs=2))
+        psum = ctx.enter_context(tc.psum_pool(name="psum", bufs=1))
         if MANUAL:
             ctx.enter_context(tc.manual_schedule())
 
         ident = keep.tile([P, P], F32, name="ident")
         haar_sb = keep.tile([P, 2048], BF16, name="haar_sb")
-        hg = keep.tile([P, 2048], BF16, name="hg", align_bytes=64)
+        hg = [keep.tile([P, 512], BF16, name="hg%d" % j, align_bytes=64) for j in range(4)]
         h1c = keep.tile([P, 512], U32, name="h1c", align_bytes=64)
         h1s = keep.tile([P, 512], U8, name="h1s", align_bytes=64)
         h2c = keep.tile([P, 256], U32, name="h2c", align_bytes=64)
         h2s = keep.tile([P, 256], U8, name="h2s", align_bytes=64)
-        xs = [keep.tile([P, 2048], BF16, name="x%d" % c) for c in range(4)]
-        gr = [keep.tile([P, 2048], BF16, name="gr%d" % c, align_bytes=64) for c in range(4)]
-        rc = [keep.tile([P, 512], U32, name="rc%d" % c, align_bytes=64) for c in range(4)]
-        rs = [keep.tile([P, 512], U8, name="rs%d" % c, align_bytes=64) for c in range(4)]
-        gt = [keep.tile([P, 2048], BF16, name="gt%d" % c, align_bytes=64) for c in range(4)]
-        tcd = [keep.tile([P, 512], U32, name="tc%d" % c, align_bytes=64) for c in range(4)]
-        tsc = [keep.tile([P, 512], U8, name="ts%d" % c, align_bytes=64) for c in range(4)]
-        ob = [keep.tile([P, 1024], F32, name="ob%d" % c) for c in range(4)]
+        xs = [keep.tile([P, 1024], BF16, name="x%d" % g) for g in range(8)]
+        gr = [keep.tile([P, 1024], BF16, name="gr%d" % g, align_bytes=64) for g in range(8)]
+        rc = [keep.tile([P, 256], U32, name="rc%d" % g, align_bytes=64) for g in range(8)]
+        rs = [keep.tile([P, 256], U8, name="rs%d" % g, align_bytes=64) for g in range(8)]
+        gt = [keep.tile([P, 512], BF16, name="gt%d" % k, align_bytes=64) for k in range(16)]
+        tcd = [keep.tile([P, 128], U32, name="tc%d" % k, align_bytes=64) for k in range(16)]
+        tsc = [keep.tile([P, 128], U8, name="ts%d" % k, align_bytes=64) for k in range(16)]
+        ob = [keep.tile([P, 512], F32, name="ob%d" % g) for g in range(8)]
+        rts = {}
+        tps = {}
+        ops = {}
 
-        def load_x(c, ch0, nch):
+        def copy_on(eng, dst, src):
+            if eng == "V":
+                nc.vector.tensor_copy(out=dst, in_=src)
+            else:
+                nc.scalar.copy(out=dst, in_=src)
+
+        def load_x(g):
+            c, h = divmod(g, 2)
             b, c2p = divmod(c, 2)
             for c2i in range(2):
                 r0 = 128 * (2 * c2p + c2i)
                 nc.sync.dma_start(
-                    out=xs[c][c2i:P:2, 512 * ch0 : 512 * (ch0 + nch)].rearrange("p (ch k) -> p ch k", ch=nch),
-                    in_=x[b, ch0 : ch0 + nch, r0 : r0 + 64, :].rearrange("ch r k -> r ch k"),
+                    out=xs[g][c2i:P:2, :].rearrange("p (ch k) -> p ch k", ch=2),
+                    in_=x[b, 2 * h : 2 * h + 2, r0 : r0 + 64, :].rearrange("ch r k -> r ch k"),
                 )
 
         def load_haar():
@@ -61,119 +67,140 @@ def tile_mylayer_kernel(tc, x, haar, out):
                 in_=haar.rearrange("(p t) n -> p t n", t=4),
             )
 
-        def prep_haar():
-            nc.vector.tensor_copy(
-                out=hg[:].rearrange("p (j c t) -> p j c t", j=4, t=4),
-                in_=haar_sb[:].rearrange("p (t c j) -> p j c t", t=4, j=4),
+        def regroup(j, eng):
+            copy_on(
+                eng,
+                hg[j][:].rearrange("p (c t) -> p c t", t=4),
+                haar_sb[:].rearrange("p (t c j) -> p j c t", t=4, j=4)[:, j],
             )
-            nc.vector.quantize_mx(out=h1c[:].bitcast(FP8X4), scales=h1s[:], in_=hg[:])
 
-        def prep_haar2():
-            for j in range(4):
-                nc.vector.quantize_mx(
-                    out=h2c[:, 64 * j : 64 * j + 64].bitcast(FP8X4),
-                    scales=h2s[:, 64 * j : 64 * j + 64],
-                    in_=hg[:, 512 * j : 512 * j + 256],
-                )
+        def quant_h1(j):
+            nc.vector.quantize_mx(
+                out=h1c[:, 128 * j : 128 * j + 128].bitcast(FP8X4),
+                scales=h1s[:, 128 * j : 128 * j + 128],
+                in_=hg[j][:],
+            )
 
-        def stage_t(g):
-            c, h = divmod(g, 2)
-            rt = ps_rt.tile([P, 2, 256], F32, name="rt")
-            xw = xs[c][:].bitcast(F32)
+        def quant_h2(j):
+            nc.vector.quantize_mx(
+                out=h2c[:, 64 * j : 64 * j + 64].bitcast(FP8X4),
+                scales=h2s[:, 64 * j : 64 * j + 64],
+                in_=hg[j][:, 0:256],
+            )
+
+        def tr(g):
+            rt = psum.tile([P, 2, 256], F32, name="rt%d" % (g % 2))
+            rts[g] = rt
+            xw = xs[g][:].bitcast(F32)
             for i in range(2):
-                ch = 2 * h + i
                 for u in range(2):
                     nc.tensor.transpose(
                         rt[:, u, 128 * i : 128 * i + 128],
-                        xw[:, 256 * ch + u : 256 * (ch + 1) : 2],
+                        xw[:, 256 * i + u : 256 * (i + 1) : 2],
                         ident[:],
                     )
-            dst = gr[c][:].bitcast(F32)[:, 512 * h : 512 * h + 512].rearrange("p (m u) -> p m u", u=2)
-            src = rt[:].rearrange("p u m -> p m u")
-            if g in ER_ON_SCALAR:
-                nc.scalar.copy(out=dst, in_=src)
-            else:
-                nc.vector.tensor_copy(out=dst, in_=src)
 
-        def quant(g, src, codes, scales):
-            c, h = divmod(g, 2)
-            nc.vector.quantize_mx(
-                out=codes[c][:, 256 * h : 256 * h + 256].bitcast(FP8X4),
-                scales=scales[c][:, 256 * h : 256 * h + 256],
-                in_=src[c][:, 1024 * h : 1024 * h + 1024],
+        def er(g, eng):
+            copy_on(
+                eng,
+                gr[g][:].bitcast(F32).rearrange("p (m u) -> p m u", u=2),
+                rts[g][:].rearrange("p u m -> p m u"),
             )
 
-        def stage_m1(g):
-            c, h = divmod(g, 2)
-            for i in range(2):
-                mo = 256 * h + 128 * i
-                tp = ps_t.tile([P, 4, 128], F32, name="tp")
-                for t in range(4):
-                    nc.tensor.matmul_mx(
-                        out=tp[:, t, :],
-                        lhsT=h1c[:, 128 * t : 128 * t + 128].bitcast(FP8X4),
-                        lhsT_scale=h1s[:, 128 * t : 128 * t + 128],
-                        rhs=rc[c][:, mo : mo + 128].bitcast(FP8X4),
-                        rhs_scale=rs[c][:, mo : mo + 128],
-                        start=True,
-                        stop=True,
-                    )
-                nc.scalar.copy(
-                    out=gt[c][:, 4 * mo : 4 * mo + 512].rearrange("p (m t) -> p m t", t=4),
-                    in_=tp[:].rearrange("p t m -> p m t"),
+        def q1(g):
+            nc.vector.quantize_mx(out=rc[g][:].bitcast(FP8X4), scales=rs[g][:], in_=gr[g][:])
+
+        def q2(g, i):
+            k = 2 * g + i
+            nc.vector.quantize_mx(out=tcd[k][:].bitcast(FP8X4), scales=tsc[k][:], in_=gt[k][:])
+
+        def m1(g, i):
+            k = 2 * g + i
+            tp = psum.tile([P, 4, 128], F32, name="tp%d" % (k % 4))
+            tps[k] = tp
+            for t in range(4):
+                nc.tensor.matmul_mx(
+                    out=tp[:, t, :],
+                    lhsT=h1c[:, 128 * t : 128 * t + 128].bitcast(FP8X4),
+                    lhsT_scale=h1s[:, 128 * t : 128 * t + 128],
+                    rhs=rc[g][:, 128 * i : 128 * i + 128].bitcast(FP8X4),
+                    rhs_scale=rs[g][:, 128 * i : 128 * i + 128],
+                    start=True,
+                    stop=True,
                 )
 
-        def stage_m2(g):
-            c, h = divmod(g, 2)
-            b, c2p = divmod(c, 2)
-            op = ps_o.tile([P, 2, 256], F32, name="op")
+        def et(g, i, eng):
+            k = 2 * g + i
+            copy_on(eng, gt[k][:].rearrange("p (m t) -> p m t", t=4), tps[k][:].rearrange("p t m -> p m t"))
+
+        def m2(g):
+            op = psum.tile([P, 2, 256], F32, name="op%d" % (g % 2))
+            ops[g] = op
             for i in range(2):
-                mo = 256 * h + 128 * i
+                k = 2 * g + i
                 nc.tensor.matmul_mx(
                     out=op[:, i, :],
-                    lhsT=tcd[c][:, mo : mo + 128].bitcast(FP8X4),
-                    lhsT_scale=tsc[c][:, mo : mo + 128],
+                    lhsT=tcd[k][:].bitcast(FP8X4),
+                    lhsT_scale=tsc[k][:],
                     rhs=h2c[:].bitcast(FP8X4),
                     rhs_scale=h2s[:],
                     start=True,
                     stop=True,
                 )
-            dst = ob[c][:, 512 * h : 512 * h + 512].rearrange("p (i c j) -> p i c j", i=2, j=4)
-            src = op[:].rearrange("p i (j c) -> p i c j", j=4)
-            if g in EO_ON_VECTOR:
-                nc.vector.tensor_copy(out=dst, in_=src)
-            else:
-                nc.scalar.copy(out=dst, in_=src)
+
+        def eo(g):
+            c, h = divmod(g, 2)
+            b, c2p = divmod(c, 2)
+            copy_on(
+                "V" if g in EO_ON_VECTOR else "S",
+                ob[g][:].rearrange("p (i c j) -> p i c j", i=2, j=4),
+                ops[g][:].rearrange("p i (j c) -> p i c j", j=4),
+            )
             for c2i in range(2):
                 nc.sync.dma_start(
                     out=out[b, 2 * c2p + c2i].rearrange("(r ch) j -> r ch j", ch=4)[:, 2 * h : 2 * h + 2, :],
-                    in_=ob[c][c2i:P:2, 512 * h : 512 * h + 512].rearrange("p (ch j) -> p ch j", ch=2),
+                    in_=ob[g][c2i:P:2, :].rearrange("p (ch j) -> p ch j", ch=2),
                 )
 
         make_identity(nc, ident[:])
-        load_x(0, 0, 2)
+        load_x(0)
         load_haar()
-        load_x(0, 2, 2)
-        for c in range(1, 4):
-            load_x(c, 0, 4)
+        for g in range(1, 8):
+            load_x(g)
 
-        stage_t(0)
-        prep_haar()
-        quant(0, gr, rc, rs)
-        stage_t(1)
-        quant(1, gr, rc, rs)
-        prep_haar2()
-        for s in range(0, 8, 2):
-            stage_m1(s)
-            stage_m1(s + 1)
-            if s + 2 < 8:
-                stage_t(s + 2)
-                stage_t(s + 3)
-            quant(s, gt, tcd, tsc)
-            if s + 2 < 8:
-                quant(s + 2, gr, rc, rs)
-            quant(s + 1, gt, tcd, tsc)
-            if s + 2 < 8:
-                quant(s + 3, gr, rc, rs)
-            stage_m2(s)
-            stage_m2(s + 1)
+        tr(0)
+        er(0, "S")
+        for j in range(4):
+            regroup(j, "S" if j >= 4 - RG_ON_SCALAR else "V")
+        for j in range(4):
+            quant_h1(j)
+        q1(0)
+        tr(1)
+        er(1, "S")
+        q1(1)
+        for j in range(4):
+            quant_h2(j)
+        tr(2)
+        er(2, "S")
+        tr(3)
+        er(3, "S")
+        for step in range(5):
+            a = 2 * step
+            if step < 4:
+                for g in (a, a + 1):
+                    m1(g, 0)
+                    et(g, 0, "S")
+                    m1(g, 1)
+                    et(g, 1, "V")
+                    q2(g, 0)
+                    if g + 2 < 8:
+                        q1(g + 2)
+                    q2(g, 1)
+            if step >= 1:
+                for g in (a - 2, a - 1):
+                    m2(g)
+                    eo(g)
+            if step < 2:
+                for g in (a + 4, a + 5):
+                    tr(g)
+                    er(g, "S")

@@ -13,7 +13,7 @@ P = 128
 FLOPS = 2 * 2048 * 512 * 512 + 2 * 2048 * 512 * 256
 BYTES = 2048 * 512 * 2 + 512 * 512 * 2 + 2048 * 256 * 4
 
-MANUAL = True
+MANUAL = False
 EO_ON_VECTOR = (0, 2, 6)
 RG_ON_SCALAR = 1
 

@@ -13,8 +13,8 @@ P = 128
 FLOPS = 2 * 2048 * 512 * 512 + 2 * 2048 * 512 * 256
 BYTES = 2048 * 512 * 2 + 512 * 512 * 2 + 2048 * 256 * 4
 
-MANUAL = False
-EO_ON_VECTOR = (0, 2, 6)
+MANUAL = True
+EO_ON_VECTOR = (0, 6)
 RG_ON_SCALAR = 1
 
 
@@ -188,13 +188,13 @@ def tile_mylayer_kernel(tc, x, haar, out):
             a = 2 * step
             if step < 4:
                 for g in (a, a + 1):
+                    if g + 2 < 8:
+                        q1(g + 2)
                     m1(g, 0)
                     et(g, 0, "S")
                     m1(g, 1)
                     et(g, 1, "V")
                     q2(g, 0)
-                    if g + 2 < 8:
-                        q1(g + 2)
                     q2(g, 1)
             if step >= 1:
                 for g in (a - 2, a - 1):

@@ -10,12 +10,16 @@ U32 = mybir.dt.uint32
 U8 = mybir.dt.uint8
 
 P = 128
-FLOPS = 2 * 2048 * 512 * 512 + 2 * 2048 * 512 * 256
-BYTES = 2048 * 512 * 2 + 512 * 512 * 2 + 2048 * 256 * 4
+PACK = 4
+K = P * PACK
+N_OUT = 256
+GRANULES = 8
+CHUNKS = 4
 
-MANUAL = True
-EO_ON_VECTOR = (0, 6)
-RG_ON_SCALAR = 1
+FLOPS = 2 * 2048 * K * K + 2 * 2048 * K * N_OUT
+BYTES = 2048 * K * 2 + K * K * 2 + 2048 * N_OUT * 4
+
+OUT_BANKS_ON_VECTOR = (0, 6)
 
 
 def tile_mylayer_kernel(tc, x, haar, out):
@@ -23,184 +27,178 @@ def tile_mylayer_kernel(tc, x, haar, out):
     with ExitStack() as ctx:
         keep = ctx.enter_context(tc.tile_pool(name="keep", bufs=1))
         psum = ctx.enter_context(tc.psum_pool(name="psum", bufs=1))
-        if MANUAL:
-            ctx.enter_context(tc.manual_schedule())
+        ctx.enter_context(tc.manual_schedule())
 
         ident = keep.tile([P, P], F32, name="ident")
-        haar_sb = keep.tile([P, 2048], BF16, name="haar_sb")
-        hg = [keep.tile([P, 512], BF16, name="hg%d" % j, align_bytes=64) for j in range(4)]
-        h1c = keep.tile([P, 512], U32, name="h1c", align_bytes=64)
-        h1s = keep.tile([P, 512], U8, name="h1s", align_bytes=64)
-        h2c = keep.tile([P, 256], U32, name="h2c", align_bytes=64)
-        h2s = keep.tile([P, 256], U8, name="h2s", align_bytes=64)
-        xs = [keep.tile([P, 1024], BF16, name="x%d" % g) for g in range(8)]
-        gr = [keep.tile([P, 1024], BF16, name="gr%d" % g, align_bytes=64) for g in range(8)]
-        rc = [keep.tile([P, 256], U32, name="rc%d" % g, align_bytes=64) for g in range(8)]
-        rs = [keep.tile([P, 256], U8, name="rs%d" % g, align_bytes=64) for g in range(8)]
-        gt = [keep.tile([P, 512], BF16, name="gt%d" % k, align_bytes=64) for k in range(16)]
-        tcd = [keep.tile([P, 128], U32, name="tc%d" % k, align_bytes=64) for k in range(16)]
-        tsc = [keep.tile([P, 128], U8, name="ts%d" % k, align_bytes=64) for k in range(16)]
-        ob = [keep.tile([P, 512], F32, name="ob%d" % g) for g in range(8)]
-        rts = {}
-        tps = {}
-        ops = {}
+        haar_rows = keep.tile([P, PACK * K], BF16, name="haar_rows")
+        haar_grouped = keep.tile([P, K * PACK], BF16, name="haar_grouped", align_bytes=64)
+        h1_codes = keep.tile([P, K], U32, name="h1_codes", align_bytes=64)
+        h1_scales = keep.tile([P, K], U8, name="h1_scales", align_bytes=64)
+        h2_codes = keep.tile([P, N_OUT], U32, name="h2_codes", align_bytes=64)
+        h2_scales = keep.tile([P, N_OUT], U8, name="h2_scales", align_bytes=64)
+        x_rows = [keep.tile([P, 2 * K], BF16, name="x%d" % g) for g in range(GRANULES)]
+        r_grouped = [keep.tile([P, 2 * P * PACK], BF16, name="rg%d" % g, align_bytes=64) for g in range(GRANULES)]
+        r_codes = [keep.tile([P, 2 * P], U32, name="rc%d" % g, align_bytes=64) for g in range(GRANULES)]
+        r_scales = [keep.tile([P, 2 * P], U8, name="rs%d" % g, align_bytes=64) for g in range(GRANULES)]
+        t_grouped = [keep.tile([P, P * PACK], BF16, name="tg%d" % u, align_bytes=64) for u in range(2 * GRANULES)]
+        t_codes = [keep.tile([P, P], U32, name="tc%d" % u, align_bytes=64) for u in range(2 * GRANULES)]
+        t_scales = [keep.tile([P, P], U8, name="ts%d" % u, align_bytes=64) for u in range(2 * GRANULES)]
+        out_rows = [keep.tile([P, 2 * N_OUT], F32, name="ob%d" % g) for g in range(GRANULES)]
+        rt_banks = {}
+        t_banks = {}
+        out_banks = {}
 
-        def copy_on(eng, dst, src):
-            if eng == "V":
-                nc.vector.tensor_copy(out=dst, in_=src)
-            else:
-                nc.scalar.copy(out=dst, in_=src)
+        def where(g):
+            c, half = divmod(g, 2)
+            b, pair = divmod(c, 2)
+            return b, 2 * pair, 2 * half
 
-        def load_x(g):
-            c, h = divmod(g, 2)
-            b, c2p = divmod(c, 2)
-            for c2i in range(2):
-                r0 = 128 * (2 * c2p + c2i)
+        def load_rows(g):
+            b, c2_first, ch_first = where(g)
+            for e in range(2):
+                row = P * (c2_first + e)
                 nc.sync.dma_start(
-                    out=xs[g][c2i:P:2, :].rearrange("p (ch k) -> p ch k", ch=2),
-                    in_=x[b, 2 * h : 2 * h + 2, r0 : r0 + 64, :].rearrange("ch r k -> r ch k"),
+                    out=x_rows[g][e:P:2, :].rearrange("p (ch k) -> p ch k", ch=2),
+                    in_=x[b, ch_first : ch_first + 2, row : row + 64, :].rearrange("ch r k -> r ch k"),
                 )
 
         def load_haar():
             nc.sync.dma_start(
-                out=haar_sb[:].rearrange("p (t n) -> p t n", t=4),
-                in_=haar.rearrange("(p t) n -> p t n", t=4),
+                out=haar_rows[:].rearrange("p (t n) -> p t n", t=PACK),
+                in_=haar.rearrange("(p t) n -> p t n", t=PACK),
             )
 
-        def regroup(j, eng):
-            copy_on(
-                eng,
-                hg[j][:].rearrange("p (c t) -> p c t", t=4),
-                haar_sb[:].rearrange("p (t c j) -> p j c t", t=4, j=4)[:, j],
+        def regroup_haar():
+            nc.vector.tensor_copy(
+                out=haar_grouped[:].rearrange("p (j c t) -> p j c t", j=4, t=PACK),
+                in_=haar_rows[:].rearrange("p (t c j) -> p j c t", t=PACK, j=4),
             )
 
-        def quant_h1(j):
-            nc.vector.quantize_mx(
-                out=h1c[:, 128 * j : 128 * j + 128].bitcast(FP8X4),
-                scales=h1s[:, 128 * j : 128 * j + 128],
-                in_=hg[j][:],
-            )
+        def quantise_haar_stationary():
+            nc.vector.quantize_mx(out=h1_codes[:].bitcast(FP8X4), scales=h1_scales[:], in_=haar_grouped[:])
 
-        def quant_h2(j):
-            nc.vector.quantize_mx(
-                out=h2c[:, 64 * j : 64 * j + 64].bitcast(FP8X4),
-                scales=h2s[:, 64 * j : 64 * j + 64],
-                in_=hg[j][:, 0:256],
-            )
+        def quantise_haar_moving():
+            for j in range(4):
+                nc.vector.quantize_mx(
+                    out=h2_codes[:, 64 * j : 64 * j + 64].bitcast(FP8X4),
+                    scales=h2_scales[:, 64 * j : 64 * j + 64],
+                    in_=haar_grouped[:, K * j : K * j + 64 * PACK],
+                )
 
-        def tr(g):
-            rt = psum.tile([P, 2, 256], F32, name="rt%d" % (g % 2))
-            rts[g] = rt
-            xw = xs[g][:].bitcast(F32)
+        def transpose_rows(g):
+            bank = psum.tile([P, 2, 2 * P], F32, name="rt%d" % (g % 2))
+            rt_banks[g] = bank
+            words = x_rows[g][:].bitcast(F32)
             for i in range(2):
-                for u in range(2):
+                for w in range(2):
                     nc.tensor.transpose(
-                        rt[:, u, 128 * i : 128 * i + 128],
-                        xw[:, 256 * i + u : 256 * (i + 1) : 2],
+                        bank[:, w, P * i : P * i + P],
+                        words[:, 256 * i + w : 256 * (i + 1) : 2],
                         ident[:],
                     )
 
-        def er(g, eng):
-            copy_on(
-                eng,
-                gr[g][:].bitcast(F32).rearrange("p (m u) -> p m u", u=2),
-                rts[g][:].rearrange("p u m -> p m u"),
+        def copy_transposed(g):
+            nc.scalar.copy(
+                out=r_grouped[g][:].bitcast(F32).rearrange("p (m w) -> p m w", w=2),
+                in_=rt_banks[g][:].rearrange("p w m -> p m w"),
             )
 
-        def q1(g):
-            nc.vector.quantize_mx(out=rc[g][:].bitcast(FP8X4), scales=rs[g][:], in_=gr[g][:])
+        def quantise_r(g):
+            nc.vector.quantize_mx(out=r_codes[g][:].bitcast(FP8X4), scales=r_scales[g][:], in_=r_grouped[g][:])
 
-        def q2(g, i):
-            k = 2 * g + i
-            nc.vector.quantize_mx(out=tcd[k][:].bitcast(FP8X4), scales=tsc[k][:], in_=gt[k][:])
-
-        def m1(g, i):
-            k = 2 * g + i
-            tp = psum.tile([P, 4, 128], F32, name="tp%d" % (k % 4))
-            tps[k] = tp
-            for t in range(4):
+        def first_matmul(g, i):
+            u = 2 * g + i
+            bank = psum.tile([P, 4, P], F32, name="tp%d" % (u % 4))
+            t_banks[u] = bank
+            for j in range(4):
                 nc.tensor.matmul_mx(
-                    out=tp[:, t, :],
-                    lhsT=h1c[:, 128 * t : 128 * t + 128].bitcast(FP8X4),
-                    lhsT_scale=h1s[:, 128 * t : 128 * t + 128],
-                    rhs=rc[g][:, 128 * i : 128 * i + 128].bitcast(FP8X4),
-                    rhs_scale=rs[g][:, 128 * i : 128 * i + 128],
+                    out=bank[:, j, :],
+                    lhsT=h1_codes[:, P * j : P * j + P].bitcast(FP8X4),
+                    lhsT_scale=h1_scales[:, P * j : P * j + P],
+                    rhs=r_codes[g][:, P * i : P * i + P].bitcast(FP8X4),
+                    rhs_scale=r_scales[g][:, P * i : P * i + P],
                     start=True,
                     stop=True,
                 )
 
-        def et(g, i, eng):
-            k = 2 * g + i
-            copy_on(eng, gt[k][:].rearrange("p (m t) -> p m t", t=4), tps[k][:].rearrange("p t m -> p m t"))
+        def copy_t(g, i):
+            u = 2 * g + i
+            copy = nc.vector.tensor_copy if i == 1 else nc.scalar.copy
+            copy(
+                out=t_grouped[u][:].rearrange("p (m j) -> p m j", j=PACK),
+                in_=t_banks[u][:].rearrange("p j m -> p m j"),
+            )
 
-        def m2(g):
-            op = psum.tile([P, 2, 256], F32, name="op%d" % (g % 2))
-            ops[g] = op
+        def quantise_t(g, i):
+            u = 2 * g + i
+            nc.vector.quantize_mx(out=t_codes[u][:].bitcast(FP8X4), scales=t_scales[u][:], in_=t_grouped[u][:])
+
+        def second_matmul(g):
+            bank = psum.tile([P, 2, N_OUT], F32, name="op%d" % (g % 2))
+            out_banks[g] = bank
             for i in range(2):
-                k = 2 * g + i
+                u = 2 * g + i
                 nc.tensor.matmul_mx(
-                    out=op[:, i, :],
-                    lhsT=tcd[k][:].bitcast(FP8X4),
-                    lhsT_scale=tsc[k][:],
-                    rhs=h2c[:].bitcast(FP8X4),
-                    rhs_scale=h2s[:],
+                    out=bank[:, i, :],
+                    lhsT=t_codes[u][:].bitcast(FP8X4),
+                    lhsT_scale=t_scales[u][:],
+                    rhs=h2_codes[:].bitcast(FP8X4),
+                    rhs_scale=h2_scales[:],
                     start=True,
                     stop=True,
                 )
 
-        def eo(g):
-            c, h = divmod(g, 2)
-            b, c2p = divmod(c, 2)
-            copy_on(
-                "V" if g in EO_ON_VECTOR else "S",
-                ob[g][:].rearrange("p (i c j) -> p i c j", i=2, j=4),
-                ops[g][:].rearrange("p i (j c) -> p i c j", j=4),
+        def copy_out(g):
+            copy = nc.vector.tensor_copy if g in OUT_BANKS_ON_VECTOR else nc.scalar.copy
+            copy(
+                out=out_rows[g][:].rearrange("p (i c j) -> p i c j", i=2, j=4),
+                in_=out_banks[g][:].rearrange("p i (j c) -> p i c j", j=4),
             )
-            for c2i in range(2):
+
+        def store(g):
+            b, c2_first, ch_first = where(g)
+            for e in range(2):
                 nc.sync.dma_start(
-                    out=out[b, 2 * c2p + c2i].rearrange("(r ch) j -> r ch j", ch=4)[:, 2 * h : 2 * h + 2, :],
-                    in_=ob[g][c2i:P:2, :].rearrange("p (ch j) -> p ch j", ch=2),
+                    out=out[b, c2_first + e].rearrange("(r ch) n -> r ch n", ch=4)[:, ch_first : ch_first + 2, :],
+                    in_=out_rows[g][e:P:2, :].rearrange("p (ch n) -> p ch n", ch=2),
                 )
 
         make_identity(nc, ident[:])
-        load_x(0)
+        load_rows(0)
         load_haar()
-        for g in range(1, 8):
-            load_x(g)
+        for g in range(1, GRANULES):
+            load_rows(g)
 
-        tr(0)
-        er(0, "S")
-        for j in range(4):
-            regroup(j, "S" if j >= 4 - RG_ON_SCALAR else "V")
-        for j in range(4):
-            quant_h1(j)
-        q1(0)
-        tr(1)
-        er(1, "S")
-        q1(1)
-        for j in range(4):
-            quant_h2(j)
-        tr(2)
-        er(2, "S")
-        tr(3)
-        er(3, "S")
-        for step in range(5):
-            a = 2 * step
-            if step < 4:
-                for g in (a, a + 1):
-                    if g + 2 < 8:
-                        q1(g + 2)
-                    m1(g, 0)
-                    et(g, 0, "S")
-                    m1(g, 1)
-                    et(g, 1, "V")
-                    q2(g, 0)
-                    q2(g, 1)
+        transpose_rows(0)
+        copy_transposed(0)
+        regroup_haar()
+        quantise_haar_stationary()
+        quantise_r(0)
+        transpose_rows(1)
+        copy_transposed(1)
+        quantise_r(1)
+        quantise_haar_moving()
+        for g in (2, 3):
+            transpose_rows(g)
+            copy_transposed(g)
+
+        for step in range(CHUNKS + 1):
+            first = 2 * step
+            if step < CHUNKS:
+                for g in (first, first + 1):
+                    if g + 2 < GRANULES:
+                        quantise_r(g + 2)
+                    for i in range(2):
+                        first_matmul(g, i)
+                        copy_t(g, i)
+                    for i in range(2):
+                        quantise_t(g, i)
             if step >= 1:
-                for g in (a - 2, a - 1):
-                    m2(g)
-                    eo(g)
-            if step < 2:
-                for g in (a + 4, a + 5):
-                    tr(g)
-                    er(g, "S")
+                for g in (first - 2, first - 1):
+                    second_matmul(g)
+                    copy_out(g)
+                    store(g)
+            for g in (first + 4, first + 5):
+                if g < GRANULES:
+                    transpose_rows(g)
+                    copy_transposed(g)

@@ -14,19 +14,18 @@ PACK = 4
 K = P * PACK
 N_OUT = 256
 GRANULES = 8
-CHUNKS = 4
+EARLY = 5
+AHEAD = 4
 
 FLOPS = 2 * 2048 * K * K + 2 * 2048 * K * N_OUT
 BYTES = 2048 * K * 2 + K * K * 2 + 2048 * N_OUT * 4
-
-OUT_BANKS_ON_VECTOR = (0, 6)
 
 
 def tile_mylayer_kernel(tc, x, haar, out):
     nc = tc.nc
     with ExitStack() as ctx:
         keep = ctx.enter_context(tc.tile_pool(name="keep", bufs=1))
-        psum = ctx.enter_context(tc.psum_pool(name="psum", bufs=1))
+        psum = ctx.enter_context(tc.psum_pool(name="psum", bufs=8))
         ctx.enter_context(tc.manual_schedule())
 
         ident = keep.tile([P, P], F32, name="ident")
@@ -40,18 +39,16 @@ def tile_mylayer_kernel(tc, x, haar, out):
         r_grouped = [keep.tile([P, 2 * P * PACK], BF16, name="rg%d" % g, align_bytes=64) for g in range(GRANULES)]
         r_codes = [keep.tile([P, 2 * P], U32, name="rc%d" % g, align_bytes=64) for g in range(GRANULES)]
         r_scales = [keep.tile([P, 2 * P], U8, name="rs%d" % g, align_bytes=64) for g in range(GRANULES)]
-        t_grouped = [keep.tile([P, P * PACK], BF16, name="tg%d" % u, align_bytes=64) for u in range(2 * GRANULES)]
-        t_codes = [keep.tile([P, P], U32, name="tc%d" % u, align_bytes=64) for u in range(2 * GRANULES)]
-        t_scales = [keep.tile([P, P], U8, name="ts%d" % u, align_bytes=64) for u in range(2 * GRANULES)]
+        t_grouped = [keep.tile([P, 2 * P * PACK], BF16, name="tg%d" % g, align_bytes=64) for g in range(GRANULES)]
+        t_codes = [keep.tile([P, 2 * P], U32, name="tc%d" % g, align_bytes=64) for g in range(GRANULES)]
+        t_scales = [keep.tile([P, 2 * P], U8, name="ts%d" % g, align_bytes=64) for g in range(GRANULES)]
         out_rows = [keep.tile([P, 2 * N_OUT], F32, name="ob%d" % g) for g in range(GRANULES)]
         rt_banks = {}
         t_banks = {}
         out_banks = {}
 
         def where(g):
-            c, half = divmod(g, 2)
-            b, pair = divmod(c, 2)
-            return b, 2 * pair, 2 * half
+            return g // 4, 2 * (g // 2 % 2), 2 * (g % 2)
 
         def load_rows(g):
             b, c2_first, ch_first = where(g)
@@ -86,7 +83,7 @@ def tile_mylayer_kernel(tc, x, haar, out):
                 )
 
         def transpose_rows(g):
-            bank = psum.tile([P, 2, 2 * P], F32, name="rt%d" % (g % 2))
+            bank = psum.tile([P, 2, 2 * P], F32, name="bank")
             rt_banks[g] = bank
             words = x_rows[g][:].bitcast(F32)
             for i in range(2):
@@ -97,8 +94,8 @@ def tile_mylayer_kernel(tc, x, haar, out):
                         ident[:],
                     )
 
-        def copy_transposed(g):
-            nc.scalar.copy(
+        def copy_transposed(copy, g):
+            copy(
                 out=r_grouped[g][:].bitcast(F32).rearrange("p (m w) -> p m w", w=2),
                 in_=rt_banks[g][:].rearrange("p w m -> p m w"),
             )
@@ -107,9 +104,8 @@ def tile_mylayer_kernel(tc, x, haar, out):
             nc.vector.quantize_mx(out=r_codes[g][:].bitcast(FP8X4), scales=r_scales[g][:], in_=r_grouped[g][:])
 
         def first_matmul(g, i):
-            u = 2 * g + i
-            bank = psum.tile([P, 4, P], F32, name="tp%d" % (u % 4))
-            t_banks[u] = bank
+            bank = psum.tile([P, 4, P], F32, name="bank")
+            t_banks[g, i] = bank
             for j in range(4):
                 nc.tensor.matmul_mx(
                     out=bank[:, j, :],
@@ -121,38 +117,39 @@ def tile_mylayer_kernel(tc, x, haar, out):
                     stop=True,
                 )
 
-        def copy_t(g, i):
-            u = 2 * g + i
-            copy = nc.vector.tensor_copy if i == 1 else nc.scalar.copy
+        def copy_t(copy, g, i):
             copy(
-                out=t_grouped[u][:].rearrange("p (m j) -> p m j", j=PACK),
-                in_=t_banks[u][:].rearrange("p j m -> p m j"),
+                out=t_grouped[g][:, K * i : K * (i + 1)].rearrange("p (m j) -> p m j", j=PACK),
+                in_=t_banks[g, i][:].rearrange("p j m -> p m j"),
             )
 
-        def quantise_t(g, i):
-            u = 2 * g + i
-            nc.vector.quantize_mx(out=t_codes[u][:].bitcast(FP8X4), scales=t_scales[u][:], in_=t_grouped[u][:])
+        def quantise_t(g, units=(0, 1)):
+            first, last = units[0], units[-1] + 1
+            nc.vector.quantize_mx(
+                out=t_codes[g][:, P * first : P * last].bitcast(FP8X4),
+                scales=t_scales[g][:, P * first : P * last],
+                in_=t_grouped[g][:, K * first : K * last],
+            )
 
-        def second_matmul(g):
-            bank = psum.tile([P, 2, N_OUT], F32, name="op%d" % (g % 2))
-            out_banks[g] = bank
-            for i in range(2):
-                u = 2 * g + i
+        def second_matmul(g, units=(0, 1)):
+            bank = psum.tile([P, 2, N_OUT], F32, name="bank")
+            for i in units:
+                out_banks[g, i] = bank
                 nc.tensor.matmul_mx(
-                    out=bank[:, i, :],
-                    lhsT=t_codes[u][:].bitcast(FP8X4),
-                    lhsT_scale=t_scales[u][:],
+                    out=bank[:, i - units[0], :],
+                    lhsT=t_codes[g][:, P * i : P * (i + 1)].bitcast(FP8X4),
+                    lhsT_scale=t_scales[g][:, P * i : P * (i + 1)],
                     rhs=h2_codes[:].bitcast(FP8X4),
                     rhs_scale=h2_scales[:],
                     start=True,
                     stop=True,
                 )
 
-        def copy_out(g):
-            copy = nc.vector.tensor_copy if g in OUT_BANKS_ON_VECTOR else nc.scalar.copy
+        def copy_out(copy, g, units=(0, 1)):
+            first, last = units[0], units[-1] + 1
             copy(
-                out=out_rows[g][:].rearrange("p (i c j) -> p i c j", i=2, j=4),
-                in_=out_banks[g][:].rearrange("p i (j c) -> p i c j", j=4),
+                out=out_rows[g][:, N_OUT * first : N_OUT * last].rearrange("p (i c j) -> p i c j", c=64, j=4),
+                in_=out_banks[g, first][:, : last - first, :].rearrange("p i (j c) -> p i c j", j=4),
             )
 
         def store(g):
@@ -169,36 +166,58 @@ def tile_mylayer_kernel(tc, x, haar, out):
         for g in range(1, GRANULES):
             load_rows(g)
 
-        transpose_rows(0)
-        copy_transposed(0)
-        regroup_haar()
-        quantise_haar_stationary()
-        quantise_r(0)
-        transpose_rows(1)
-        copy_transposed(1)
-        quantise_r(1)
-        quantise_haar_moving()
-        for g in (2, 3):
+        scalar_copy, vector_copy = nc.scalar.copy, nc.vector.tensor_copy
+        for g in range(EARLY):
             transpose_rows(g)
-            copy_transposed(g)
+            copy_transposed(scalar_copy, g)
+            if g == 0:
+                regroup_haar()
+                quantise_r(0)
+                quantise_haar_stationary()
+                quantise_haar_moving()
+            elif g < 4:
+                quantise_r(g)
 
-        for step in range(CHUNKS + 1):
-            first = 2 * step
-            if step < CHUNKS:
-                for g in (first, first + 1):
-                    if g + 2 < GRANULES:
-                        quantise_r(g + 2)
-                    for i in range(2):
-                        first_matmul(g, i)
-                        copy_t(g, i)
-                    for i in range(2):
-                        quantise_t(g, i)
-            if step >= 1:
-                for g in (first - 2, first - 1):
-                    second_matmul(g)
-                    copy_out(g)
-                    store(g)
-            for g in (first + 4, first + 5):
-                if g < GRANULES:
-                    transpose_rows(g)
-                    copy_transposed(g)
+        for g in range(AHEAD):
+            for i in range(2):
+                first_matmul(g, i)
+            copy_t(scalar_copy, g, 0)
+            copy_t(vector_copy, g, 1)
+            if g == 0:
+                quantise_r(4)
+            else:
+                quantise_t(g - 1)
+
+        for g in range(EARLY, GRANULES):
+            transpose_rows(g)
+        copy_transposed(scalar_copy, 5)
+        quantise_r(5)
+        copy_transposed(scalar_copy, 6)
+        copy_transposed(vector_copy, 7)
+        quantise_t(3)
+        quantise_r(6)
+
+        for g in range(AHEAD):
+            second_matmul(g)
+            for i in range(2):
+                first_matmul(g + AHEAD, i)
+            copy_out(scalar_copy, g)
+            store(g)
+            copy_t(scalar_copy, g + AHEAD, 0)
+            copy_t(vector_copy, g + AHEAD, 1)
+            if g == 0:
+                quantise_r(7)
+            else:
+                quantise_t(g + AHEAD - 1)
+
+        for g in (4, 5, 6):
+            second_matmul(g)
+            copy_out(scalar_copy, g)
+            store(g)
+            if g == 4:
+                quantise_t(7, (0,))
+                quantise_t(7, (1,))
+        for i, copy in enumerate((scalar_copy, vector_copy)):
+            second_matmul(7, (i,))
+            copy_out(copy, 7, (i,))
+        store(7)

@@ -29,6 +29,8 @@ def tile_mylayer_kernel(tc, x, haar, out):
         ctx.enter_context(tc.manual_schedule())
 
         ident = keep.tile([P, P], F32, name="ident")
+        zeros = keep.tile([P, K], BF16, name="zeros")
+        warm_bank = psum.tile([P, K], F32, name="bank")
         haar_rows = keep.tile([P, PACK * K], BF16, name="haar_rows")
         haar_grouped = keep.tile([P, K * PACK], BF16, name="haar_grouped", align_bytes=64)
         h1_codes = keep.tile([P, K], U32, name="h1_codes", align_bytes=64)
@@ -160,16 +162,24 @@ def tile_mylayer_kernel(tc, x, haar, out):
                     in_=out_rows[g][e:P:2, :].rearrange("p (ch n) -> p ch n", ch=2),
                 )
 
+        def warm_up(count):
+            for k in range(count):
+                nc.tensor.matmul(warm_bank[:], lhsT=zeros[:, :P], rhs=zeros[:], start=True, stop=True)
+
         make_identity(nc, ident[:])
         load_rows(0)
         load_haar()
         for g in range(1, GRANULES):
             load_rows(g)
 
+        nc.vector.memset(zeros[:], 0.0)
+        warm_up(4)
         scalar_copy, vector_copy = nc.scalar.copy, nc.vector.tensor_copy
         for g in range(EARLY):
             transpose_rows(g)
             copy_transposed(scalar_copy, g)
+            if g < 4:
+                warm_up(1)
             if g == 0:
                 regroup_haar()
                 quantise_r(0)

@@ -7,6 +7,7 @@ FP8X4 = mybir.dt.float8_e4m3fn_x4
 BF16 = mybir.dt.bfloat16
 F32 = mybir.dt.float32
 U32 = mybir.dt.uint32
+I32 = mybir.dt.int32
 U8 = mybir.dt.uint8
 
 P = 128
@@ -67,21 +68,20 @@ def tile_mylayer_kernel(tc, x, haar, out):
                 in_=haar.rearrange("(p t) n -> p t n", t=PACK),
             )
 
-        def regroup_haar():
-            nc.vector.tensor_copy(
-                out=haar_grouped[:].rearrange("p (j c t) -> p j c t", j=4, t=PACK),
-                in_=haar_rows[:].rearrange("p (t c j) -> p j c t", t=PACK, j=4),
+        def regroup_haar(copy, first, last):
+            copy(
+                out=haar_grouped[:, K * first : K * last].rearrange("p (j c t) -> p j c t", j=last - first, t=PACK),
+                in_=haar_rows[:].rearrange("p (t c j) -> p j c t", t=PACK, j=4)[:, first:last],
             )
 
         def quantise_haar_stationary():
             nc.vector.quantize_mx(out=h1_codes[:].bitcast(FP8X4), scales=h1_scales[:], in_=haar_grouped[:])
 
-        def quantise_haar_moving():
-            for j in range(4):
-                nc.vector.quantize_mx(
-                    out=h2_codes[:, 64 * j : 64 * j + 64].bitcast(FP8X4),
-                    scales=h2_scales[:, 64 * j : 64 * j + 64],
-                    in_=haar_grouped[:, K * j : K * j + 64 * PACK],
+        def pick_haar_moving():
+            for moving, stationary, width in ((h2_codes, h1_codes, P), (h2_scales, h1_scales, P // PACK)):
+                nc.vector.tensor_copy(
+                    out=moving[:].bitcast(I32).rearrange("p (j c) -> p j c", j=4),
+                    in_=stationary[:].bitcast(I32).rearrange("p (j c) -> p j c", j=4)[:, :, : width // 2],
                 )
 
         def transpose_rows(g):
@@ -173,20 +173,24 @@ def tile_mylayer_kernel(tc, x, haar, out):
             load_rows(g)
 
         nc.vector.memset(zeros[:], 0.0)
-        warm_up(4)
+        nc.vector.memset(h1_scales[:].bitcast(I32), 0)
+        warm_up(3)
         scalar_copy, vector_copy = nc.scalar.copy, nc.vector.tensor_copy
         for g in range(EARLY):
             transpose_rows(g)
             copy_transposed(scalar_copy, g)
-            if g < 4:
-                warm_up(1)
+            if g < 2:
+                warm_up(2 - g)
             if g == 0:
-                regroup_haar()
+                regroup_haar(vector_copy, 0, 2)
+                regroup_haar(scalar_copy, 3, 4)
+                regroup_haar(vector_copy, 2, 3)
                 quantise_r(0)
                 quantise_haar_stationary()
-                quantise_haar_moving()
             elif g < 4:
                 quantise_r(g)
+                if g == 1:
+                    pick_haar_moving()
 
         for g in range(AHEAD):
             for i in range(2):
@@ -214,10 +218,12 @@ def tile_mylayer_kernel(tc, x, haar, out):
             copy_out(scalar_copy, g)
             store(g)
             copy_t(scalar_copy, g + AHEAD, 0)
+            if g == AHEAD - 1:
+                quantise_t(6)
             copy_t(vector_copy, g + AHEAD, 1)
             if g == 0:
                 quantise_r(7)
-            else:
+            elif g < AHEAD - 1:
                 quantise_t(g + AHEAD - 1)
 
         for g in (4, 5, 6):

@@ -15,7 +15,7 @@ PACK = 4
 K = P * PACK
 N_OUT = 256
 GRANULES = 8
-EARLY = 5
+EARLY = 4
 AHEAD = 4
 
 FLOPS = 2 * 2048 * K * K + 2 * 2048 * K * N_OUT
@@ -96,8 +96,8 @@ def tile_mylayer_kernel(tc, x, haar, out):
                         ident[:],
                     )
 
-        def copy_transposed(copy, g):
-            copy(
+        def copy_transposed(g):
+            nc.scalar.copy(
                 out=r_grouped[g][:].bitcast(F32).rearrange("p (m w) -> p m w", w=2),
                 in_=rt_banks[g][:].rearrange("p w m -> p m w"),
             )
@@ -172,50 +172,48 @@ def tile_mylayer_kernel(tc, x, haar, out):
         for g in range(1, GRANULES):
             load_rows(g)
 
-        nc.vector.memset(zeros[:], 0.0)
+        nc.vector.memset(zeros[:].bitcast(F32), 0.0)
         nc.vector.memset(h1_scales[:].bitcast(I32), 0)
-        warm_up(3)
+        warm_up(4)
         scalar_copy, vector_copy = nc.scalar.copy, nc.vector.tensor_copy
         for g in range(EARLY):
             transpose_rows(g)
-            copy_transposed(scalar_copy, g)
-            if g < 2:
-                warm_up(2 - g)
+            copy_transposed(g)
+            if g < 3:
+                warm_up((2, 1, 1)[g])
             if g == 0:
                 regroup_haar(vector_copy, 0, 2)
                 regroup_haar(scalar_copy, 3, 4)
                 regroup_haar(vector_copy, 2, 3)
                 quantise_r(0)
                 quantise_haar_stationary()
-            elif g < 4:
-                quantise_r(g)
-                if g == 1:
-                    pick_haar_moving()
+            if g == 1:
+                quantise_r(1)
+                pick_haar_moving()
+            if g == 2:
+                quantise_r(2)
 
         for g in range(AHEAD):
             for i in range(2):
                 first_matmul(g, i)
             copy_t(scalar_copy, g, 0)
             copy_t(vector_copy, g, 1)
-            if g == 0:
-                quantise_r(4)
-            else:
+            if g >= 1:
                 quantise_t(g - 1)
-
-        for g in range(EARLY, GRANULES):
-            transpose_rows(g)
-        copy_transposed(scalar_copy, 5)
-        quantise_r(5)
-        copy_transposed(scalar_copy, 6)
-        copy_transposed(vector_copy, 7)
+            if g % 2 == 0:
+                quantise_r(g + 3)
+            else:
+                for later in (g + 3, g + 4):
+                    transpose_rows(later)
+                    copy_transposed(later)
+                quantise_r(g + 3)
         quantise_t(3)
-        quantise_r(6)
 
         for g in range(AHEAD):
             second_matmul(g)
             for i in range(2):
                 first_matmul(g + AHEAD, i)
-            copy_out(scalar_copy, g)
+            copy_out(vector_copy if g == 3 else scalar_copy, g)
             store(g)
             copy_t(scalar_copy, g + AHEAD, 0)
             if g == AHEAD - 1:

@@ -179,8 +179,8 @@ def tile_mylayer_kernel(tc, x, haar, out):
         for g in range(EARLY):
             transpose_rows(g)
             copy_transposed(g)
-            if g < 3:
-                warm_up((2, 1, 1)[g])
+            if g < 2:
+                warm_up((3, 1)[g])
             if g == 0:
                 regroup_haar(vector_copy, 0, 2)
                 regroup_haar(scalar_copy, 3, 4)

@@ -53,13 +53,14 @@ def tile_mylayer_kernel(tc, x, haar, out):
         def where(g):
             return g // 4, 2 * (g // 2 % 2), 2 * (g % 2)
 
-        def load_rows(g):
+        def load_rows(g, units=(0, 1)):
             b, c2_first, ch_first = where(g)
+            first, last = units[0], units[-1] + 1
             for e in range(2):
                 row = P * (c2_first + e)
                 nc.sync.dma_start(
-                    out=x_rows[g][e:P:2, :].rearrange("p (ch k) -> p ch k", ch=2),
-                    in_=x[b, ch_first : ch_first + 2, row : row + 64, :].rearrange("ch r k -> r ch k"),
+                    out=x_rows[g][e:P:2, K * first : K * last].rearrange("p (ch k) -> p ch k", ch=last - first),
+                    in_=x[b, ch_first + first : ch_first + last, row : row + 64, :].rearrange("ch r k -> r ch k"),
                 )
 
         def load_haar():
@@ -74,21 +75,25 @@ def tile_mylayer_kernel(tc, x, haar, out):
                 in_=haar_rows[:].rearrange("p (t c j) -> p j c t", t=PACK, j=4)[:, first:last],
             )
 
-        def quantise_haar_stationary():
-            nc.vector.quantize_mx(out=h1_codes[:].bitcast(FP8X4), scales=h1_scales[:], in_=haar_grouped[:])
+        def quantise_haar(first, last):
+            nc.vector.quantize_mx(
+                out=h1_codes[:, P * first : P * last].bitcast(FP8X4),
+                scales=h1_scales[:, P * first : P * last],
+                in_=haar_grouped[:, K * first : K * last],
+            )
 
         def pick_haar_moving():
             for moving, stationary, width in ((h2_codes, h1_codes, P), (h2_scales, h1_scales, P // PACK)):
-                nc.vector.tensor_copy(
+                nc.sync.dma_start(
                     out=moving[:].bitcast(I32).rearrange("p (j c) -> p j c", j=4),
                     in_=stationary[:].bitcast(I32).rearrange("p (j c) -> p j c", j=4)[:, :, : width // 2],
                 )
 
-        def transpose_rows(g):
+        def transpose_rows(g, units=(0, 1)):
             bank = psum.tile([P, 2, 2 * P], F32, name="bank")
-            rt_banks[g] = bank
+            rt_banks[g, units[0]] = bank
             words = x_rows[g][:].bitcast(F32)
-            for i in range(2):
+            for i in units:
                 for w in range(2):
                     nc.tensor.transpose(
                         bank[:, w, P * i : P * i + P],
@@ -96,14 +101,20 @@ def tile_mylayer_kernel(tc, x, haar, out):
                         ident[:],
                     )
 
-        def copy_transposed(g):
-            nc.scalar.copy(
-                out=r_grouped[g][:].bitcast(F32).rearrange("p (m w) -> p m w", w=2),
-                in_=rt_banks[g][:].rearrange("p w m -> p m w"),
+        def copy_transposed(copy, g, units=(0, 1)):
+            first, last = units[0], units[-1] + 1
+            copy(
+                out=r_grouped[g][:, K * first : K * last].bitcast(F32).rearrange("p (m w) -> p m w", w=2),
+                in_=rt_banks[g, first][:, :, P * first : P * last].rearrange("p w m -> p m w"),
             )
 
-        def quantise_r(g):
-            nc.vector.quantize_mx(out=r_codes[g][:].bitcast(FP8X4), scales=r_scales[g][:], in_=r_grouped[g][:])
+        def quantise_r(g, units=(0, 1)):
+            first, last = units[0], units[-1] + 1
+            nc.vector.quantize_mx(
+                out=r_codes[g][:, P * first : P * last].bitcast(FP8X4),
+                scales=r_scales[g][:, P * first : P * last],
+                in_=r_grouped[g][:, K * first : K * last],
+            )
 
         def first_matmul(g, i):
             bank = psum.tile([P, 4, P], F32, name="bank")
@@ -178,7 +189,7 @@ def tile_mylayer_kernel(tc, x, haar, out):
         scalar_copy, vector_copy = nc.scalar.copy, nc.vector.tensor_copy
         for g in range(EARLY):
             transpose_rows(g)
-            copy_transposed(g)
+            copy_transposed(scalar_copy, g)
             if g < 2:
                 warm_up((3, 1)[g])
             if g == 0:
@@ -186,49 +197,54 @@ def tile_mylayer_kernel(tc, x, haar, out):
                 regroup_haar(scalar_copy, 3, 4)
                 regroup_haar(vector_copy, 2, 3)
                 quantise_r(0)
-                quantise_haar_stationary()
+                quantise_haar(0, 4)
             if g == 1:
                 quantise_r(1)
                 pick_haar_moving()
             if g == 2:
                 quantise_r(2)
 
-        for g in range(AHEAD):
+        def first_product(g):
             for i in range(2):
                 first_matmul(g, i)
-            copy_t(scalar_copy, g, 0)
-            copy_t(vector_copy, g, 1)
-            if g >= 1:
-                quantise_t(g - 1)
-            if g % 2 == 0:
-                quantise_r(g + 3)
+
+        def empty_t(g):
+            on_vector = {2: (), 7: (0, 1)}.get(g, (0,) if g % 3 == 0 else (1,))
+            for i in range(2):
+                copy_t(vector_copy if i in on_vector else scalar_copy, g, i)
+
+        for g in range(AHEAD):
+            first_product(g)
+            empty_t(g)
+            if g == 0:
+                quantise_r(3)
             else:
-                for later in (g + 3, g + 4):
-                    transpose_rows(later)
-                    copy_transposed(later)
-                quantise_r(g + 3)
-        quantise_t(3)
+                quantise_t(g - 1)
+        for g in range(EARLY, GRANULES):
+            transpose_rows(g)
+            copy_transposed(vector_copy if g == 5 else scalar_copy, g)
+            if g > EARLY:
+                quantise_r(g - 1)
+            if g == 6:
+                quantise_t(3)
+        quantise_r(7)
 
         for g in range(AHEAD):
             second_matmul(g)
-            for i in range(2):
-                first_matmul(g + AHEAD, i)
-            copy_out(vector_copy if g == 3 else scalar_copy, g)
+            copy_out(scalar_copy, g)
             store(g)
-            copy_t(scalar_copy, g + AHEAD, 0)
+            first_product(g + AHEAD)
             if g == AHEAD - 1:
                 quantise_t(6)
-            copy_t(vector_copy, g + AHEAD, 1)
-            if g == 0:
-                quantise_r(7)
-            elif g < AHEAD - 1:
+            empty_t(g + AHEAD)
+            if 0 < g < AHEAD - 1:
                 quantise_t(g + AHEAD - 1)
 
         for g in (4, 5, 6):
             second_matmul(g)
             copy_out(scalar_copy, g)
             store(g)
-            if g == 4:
+            if g == 5:
                 quantise_t(7, (0,))
                 quantise_t(7, (1,))
         for i, copy in enumerate((scalar_copy, vector_copy)):

@@ -208,9 +208,9 @@ def tile_mylayer_kernel(tc, x, haar, out):
             for i in range(2):
                 first_matmul(g, i)
 
-        def empty_t(g):
+        def empty_t(g, units=(0, 1)):
             on_vector = {2: (), 7: (0, 1)}.get(g, (0,) if g % 3 == 0 else (1,))
-            for i in range(2):
+            for i in units:
                 copy_t(vector_copy if i in on_vector else scalar_copy, g, i)
 
         for g in range(AHEAD):
@@ -234,11 +234,12 @@ def tile_mylayer_kernel(tc, x, haar, out):
             copy_out(scalar_copy, g)
             store(g)
             first_product(g + AHEAD)
-            if g == AHEAD - 1:
-                quantise_t(6)
-            empty_t(g + AHEAD)
-            if 0 < g < AHEAD - 1:
+            empty_t(g + AHEAD, (0,))
+            if g > 1:
                 quantise_t(g + AHEAD - 1)
+            empty_t(g + AHEAD, (1,))
+            if g == 1:
+                quantise_t(4)
 
         for g in (4, 5, 6):
             second_matmul(g)

@@ -16,7 +16,7 @@ K = P * PACK
 N_OUT = 256
 GRANULES = 8
 EARLY = 4
-AHEAD = 4
+AHEAD = 3
 
 FLOPS = 2 * 2048 * K * K + 2 * 2048 * K * N_OUT
 BYTES = 2048 * K * 2 + K * K * 2 + 2048 * N_OUT * 4
@@ -204,14 +204,26 @@ def tile_mylayer_kernel(tc, x, haar, out):
             if g == 2:
                 quantise_r(2)
 
+        vector_t = ((0, 1), (2, 0), (5, 1), (7, 0))
+        vector_rt = (5, 6)
+        vector_out = (1, 2, 5)
+
         def first_product(g):
             for i in range(2):
                 first_matmul(g, i)
 
         def empty_t(g, units=(0, 1)):
-            on_vector = {2: (), 7: (0, 1)}.get(g, (0,) if g % 3 == 0 else (1,))
             for i in units:
-                copy_t(vector_copy if i in on_vector else scalar_copy, g, i)
+                copy_t(vector_copy if (g, i) in vector_t else scalar_copy, g, i)
+
+        def transposes(g):
+            transpose_rows(g)
+            copy_transposed(vector_copy if g in vector_rt else scalar_copy, g)
+
+        def second_product(g):
+            second_matmul(g)
+            copy_out(vector_copy if g in vector_out else scalar_copy, g)
+            store(g)
 
         for g in range(AHEAD):
             first_product(g)
@@ -220,35 +232,36 @@ def tile_mylayer_kernel(tc, x, haar, out):
                 quantise_r(3)
             else:
                 quantise_t(g - 1)
-        for g in range(EARLY, GRANULES):
-            transpose_rows(g)
-            copy_transposed(vector_copy if g == 5 else scalar_copy, g)
-            if g > EARLY:
-                quantise_r(g - 1)
-            if g == 6:
-                quantise_t(3)
+        transposes(4)
+        transposes(5)
+        quantise_r(4)
+        quantise_t(2)
+        quantise_r(5)
+        first_product(3)
+        empty_t(3)
+        second_product(0)
+        transposes(6)
+        transposes(7)
+        quantise_t(3)
+        quantise_r(6)
         quantise_r(7)
 
-        for g in range(AHEAD):
-            second_matmul(g)
-            copy_out(scalar_copy, g)
-            store(g)
-            first_product(g + AHEAD)
-            empty_t(g + AHEAD, (0,))
-            if g > 1:
-                quantise_t(g + AHEAD - 1)
-            empty_t(g + AHEAD, (1,))
-            if g == 1:
-                quantise_t(4)
-
-        for g in (4, 5, 6):
-            second_matmul(g)
-            copy_out(scalar_copy, g)
-            store(g)
-            if g == 5:
-                quantise_t(7, (0,))
-                quantise_t(7, (1,))
-        for i, copy in enumerate((scalar_copy, vector_copy)):
+        for g in range(4, GRANULES):
+            first_product(g)
+            empty_t(g, (0,))
+            if g == 7:
+                second_product(4)
+                quantise_t(6)
+            empty_t(g, (1,))
+            if g in (5, 6):
+                quantise_t(g - 1)
+            if g < 7:
+                second_product(g - AHEAD)
+        second_product(5)
+        quantise_t(7, (0,))
+        quantise_t(7, (1,))
+        second_product(6)
+        for i, copy in enumerate((vector_copy, scalar_copy)):
             second_matmul(7, (i,))
             copy_out(copy, 7, (i,))
         store(7)

from contextlib import ExitStack

import concourse.mybir as mybir
from concourse.masks import make_identity

FP8X4 = mybir.dt.float8_e4m3fn_x4
BF16 = mybir.dt.bfloat16
F32 = mybir.dt.float32
U32 = mybir.dt.uint32
I32 = mybir.dt.int32
U8 = mybir.dt.uint8

P = 128
PACK = 4
K = P * PACK
N_OUT = 256
GRANULES = 8
EARLY = 4
AHEAD = 3

FLOPS = 2 * 2048 * K * K + 2 * 2048 * K * N_OUT
BYTES = 2048 * K * 2 + K * K * 2 + 2048 * N_OUT * 4


def tile_mylayer_kernel(tc, x, haar, out):
    nc = tc.nc
    with ExitStack() as ctx:
        keep = ctx.enter_context(tc.tile_pool(name="keep", bufs=1))
        psum = ctx.enter_context(tc.psum_pool(name="psum", bufs=8))
        ctx.enter_context(tc.manual_schedule())

        ident = keep.tile([P, P], F32, name="ident")
        zeros = keep.tile([P, K], BF16, name="zeros")
        warm_bank = psum.tile([P, K], F32, name="bank")
        haar_rows = keep.tile([P, PACK * K], BF16, name="haar_rows")
        haar_grouped = keep.tile([P, K * PACK], BF16, name="haar_grouped", align_bytes=64)
        h1_codes = keep.tile([P, K], U32, name="h1_codes", align_bytes=64)
        h1_scales = keep.tile([P, K], U8, name="h1_scales", align_bytes=64)
        h2_codes = keep.tile([P, N_OUT], U32, name="h2_codes", align_bytes=64)
        h2_scales = keep.tile([P, N_OUT], U8, name="h2_scales", align_bytes=64)
        x_rows = [keep.tile([P, 2 * K], BF16, name="x%d" % g) for g in range(GRANULES)]
        r_grouped = [keep.tile([P, 2 * P * PACK], BF16, name="rg%d" % g, align_bytes=64) for g in range(GRANULES)]
        r_codes = [keep.tile([P, 2 * P], U32, name="rc%d" % g, align_bytes=64) for g in range(GRANULES)]
        r_scales = [keep.tile([P, 2 * P], U8, name="rs%d" % g, align_bytes=64) for g in range(GRANULES)]
        t_grouped = [keep.tile([P, 2 * P * PACK], BF16, name="tg%d" % g, align_bytes=64) for g in range(GRANULES)]
        t_codes = [keep.tile([P, 2 * P], U32, name="tc%d" % g, align_bytes=64) for g in range(GRANULES)]
        t_scales = [keep.tile([P, 2 * P], U8, name="ts%d" % g, align_bytes=64) for g in range(GRANULES)]
        out_rows = [keep.tile([P, 2 * N_OUT], F32, name="ob%d" % g) for g in range(GRANULES)]
        rt_banks = {}
        t_banks = {}
        out_banks = {}

        def where(g):
            return g // 4, 2 * (g // 2 % 2), 2 * (g % 2)

        def load_rows(g, units=(0, 1)):
            b, c2_first, ch_first = where(g)
            first, last = units[0], units[-1] + 1
            for e in range(2):
                row = P * (c2_first + e)
                nc.sync.dma_start(
                    out=x_rows[g][e:P:2, K * first : K * last].rearrange("p (ch k) -> p ch k", ch=last - first),
                    in_=x[b, ch_first + first : ch_first + last, row : row + 64, :].rearrange("ch r k -> r ch k"),
                )

        def load_haar():
            nc.sync.dma_start(
                out=haar_rows[:].rearrange("p (t n) -> p t n", t=PACK),
                in_=haar.rearrange("(p t) n -> p t n", t=PACK),
            )

        def regroup_haar(copy, first, last):
            copy(
                out=haar_grouped[:, K * first : K * last].rearrange("p (j c t) -> p j c t", j=last - first, t=PACK),
                in_=haar_rows[:].rearrange("p (t c j) -> p j c t", t=PACK, j=4)[:, first:last],
            )

        def quantise_haar(first, last):
            nc.vector.quantize_mx(
                out=h1_codes[:, P * first : P * last].bitcast(FP8X4),
                scales=h1_scales[:, P * first : P * last],
                in_=haar_grouped[:, K * first : K * last],
            )

        def pick_haar_moving():
            for moving, stationary, width in ((h2_codes, h1_codes, P), (h2_scales, h1_scales, P // PACK)):
                nc.sync.dma_start(
                    out=moving[:].bitcast(I32).rearrange("p (j c) -> p j c", j=4),
                    in_=stationary[:].bitcast(I32).rearrange("p (j c) -> p j c", j=4)[:, :, : width // 2],
                )

        def transpose_rows(g, units=(0, 1)):
            bank = psum.tile([P, 2, 2 * P], F32, name="bank")
            rt_banks[g, units[0]] = bank
            words = x_rows[g][:].bitcast(F32)
            for i in units:
                for w in range(2):
                    nc.tensor.transpose(
                        bank[:, w, P * i : P * i + P],
                        words[:, 256 * i + w : 256 * (i + 1) : 2],
                        ident[:],
                    )

        def copy_transposed(copy, g, units=(0, 1)):
            first, last = units[0], units[-1] + 1
            copy(
                out=r_grouped[g][:, K * first : K * last].bitcast(F32).rearrange("p (m w) -> p m w", w=2),
                in_=rt_banks[g, first][:, :, P * first : P * last].rearrange("p w m -> p m w"),
            )

        def quantise_r(g, units=(0, 1)):
            first, last = units[0], units[-1] + 1
            nc.vector.quantize_mx(
                out=r_codes[g][:, P * first : P * last].bitcast(FP8X4),
                scales=r_scales[g][:, P * first : P * last],
                in_=r_grouped[g][:, K * first : K * last],
            )

        def first_matmul(g, i):
            bank = psum.tile([P, 4, P], F32, name="bank")
            t_banks[g, i] = bank
            for j in range(4):
                nc.tensor.matmul_mx(
                    out=bank[:, j, :],
                    lhsT=h1_codes[:, P * j : P * j + P].bitcast(FP8X4),
                    lhsT_scale=h1_scales[:, P * j : P * j + P],
                    rhs=r_codes[g][:, P * i : P * i + P].bitcast(FP8X4),
                    rhs_scale=r_scales[g][:, P * i : P * i + P],
                    start=True,
                    stop=True,
                )

        def copy_t(copy, g, i):
            copy(
                out=t_grouped[g][:, K * i : K * (i + 1)].rearrange("p (m j) -> p m j", j=PACK),
                in_=t_banks[g, i][:].rearrange("p j m -> p m j"),
            )

        def quantise_t(g, units=(0, 1)):
            first, last = units[0], units[-1] + 1
            nc.vector.quantize_mx(
                out=t_codes[g][:, P * first : P * last].bitcast(FP8X4),
                scales=t_scales[g][:, P * first : P * last],
                in_=t_grouped[g][:, K * first : K * last],
            )

        def second_matmul(g, units=(0, 1)):
            bank = psum.tile([P, 2, N_OUT], F32, name="bank")
            for i in units:
                out_banks[g, i] = bank
                nc.tensor.matmul_mx(
                    out=bank[:, i - units[0], :],
                    lhsT=t_codes[g][:, P * i : P * (i + 1)].bitcast(FP8X4),
                    lhsT_scale=t_scales[g][:, P * i : P * (i + 1)],
                    rhs=h2_codes[:].bitcast(FP8X4),
                    rhs_scale=h2_scales[:],
                    start=True,
                    stop=True,
                )

        def copy_out(copy, g, units=(0, 1)):
            first, last = units[0], units[-1] + 1
            copy(
                out=out_rows[g][:, N_OUT * first : N_OUT * last].rearrange("p (i c j) -> p i c j", c=64, j=4),
                in_=out_banks[g, first][:, : last - first, :].rearrange("p i (j c) -> p i c j", j=4),
            )

        def store(g):
            b, c2_first, ch_first = where(g)
            for e in range(2):
                nc.sync.dma_start(
                    out=out[b, c2_first + e].rearrange("(r ch) n -> r ch n", ch=4)[:, ch_first : ch_first + 2, :],
                    in_=out_rows[g][e:P:2, :].rearrange("p (ch n) -> p ch n", ch=2),
                )

        def warm_up(count):
            for k in range(count):
                nc.tensor.matmul(warm_bank[:], lhsT=zeros[:, :P], rhs=zeros[:], start=True, stop=True)

        make_identity(nc, ident[:])
        load_rows(0)
        load_haar()
        for g in range(1, GRANULES):
            load_rows(g)

        nc.vector.memset(zeros[:].bitcast(F32), 0.0)
        nc.vector.memset(h1_scales[:].bitcast(I32), 0)
        warm_up(4)
        scalar_copy, vector_copy = nc.scalar.copy, nc.vector.tensor_copy
        for g in range(EARLY):
            transpose_rows(g)
            copy_transposed(scalar_copy, g)
            if g < 2:
                warm_up((3, 1)[g])
            if g == 0:
                regroup_haar(vector_copy, 0, 2)
                regroup_haar(scalar_copy, 3, 4)
                regroup_haar(vector_copy, 2, 3)
                quantise_r(0)
                quantise_haar(0, 4)
            if g == 1:
                quantise_r(1)
                pick_haar_moving()
            if g == 2:
                quantise_r(2)

        vector_t = ((0, 1), (2, 0), (5, 1), (7, 0))
        vector_rt = (5, 6)
        vector_out = (1, 2, 5)

        def first_product(g):
            for i in range(2):
                first_matmul(g, i)

        def empty_t(g, units=(0, 1)):
            for i in units:
                copy_t(vector_copy if (g, i) in vector_t else scalar_copy, g, i)

        def transposes(g):
            transpose_rows(g)
            copy_transposed(vector_copy if g in vector_rt else scalar_copy, g)

        def second_product(g):
            second_matmul(g)
            copy_out(vector_copy if g in vector_out else scalar_copy, g)
            store(g)

        for g in range(AHEAD):
            first_product(g)
            empty_t(g)
            if g == 0:
                quantise_r(3)
            else:
                quantise_t(g - 1)
        transposes(4)
        transposes(5)
        quantise_r(4)
        quantise_t(2)
        quantise_r(5)
        first_product(3)
        empty_t(3)
        second_product(0)
        transposes(6)
        transposes(7)
        quantise_t(3)
        quantise_r(6)
        quantise_r(7)

        for g in range(4, GRANULES):
            first_product(g)
            empty_t(g, (0,))
            if g == 7:
                second_product(4)
                quantise_t(6)
            empty_t(g, (1,))
            if g in (5, 6):
                quantise_t(g - 1)
            if g < 7:
                second_product(g - AHEAD)
        second_product(5)
        quantise_t(7, (0,))
        quantise_t(7, (1,))
        second_product(6)
        for i, copy in enumerate((vector_copy, scalar_copy)):
            second_matmul(7, (i,))
            copy_out(copy, 7, (i,))
        store(7)
